import numpy as np
import ml_dtypes


def mxq(x, axis, fmt="e4m3"):
    dtype, down = {"e4m3": (ml_dtypes.float8_e4m3fn, 7), "e5m2": (ml_dtypes.float8_e5m2, 14)}[fmt]
    v = np.moveaxis(np.asarray(x, np.float32).astype(ml_dtypes.bfloat16).astype(np.float64), axis, -1)
    blocks = v.reshape(v.shape[:-1] + (-1, 32))
    amax = np.abs(blocks).max(-1, keepdims=True)
    byte = np.maximum(np.where(amax > 0, np.frexp(amax)[1] - 1 + 127, 0) - down, 1)
    scale = np.exp2(byte - 127.0)
    codes = (blocks / scale).astype(np.float32).astype(dtype).astype(np.float64)
    return np.moveaxis((codes * scale).reshape(v.shape), -1, axis)


WIDE = False


def mx_kscale(k):
    if not WIDE:
        return np.ones(k)
    levels = np.array([10, -10, 5, -5, 0])
    a = np.random.permutation(np.resize(levels, k // 512 * 4)).reshape(k // 512, 4)
    idx = np.arange(k)
    return np.exp2(a[idx // 512, idx % 128 // 32])


BF16 = ml_dtypes.bfloat16


def bf(x):
    return np.asarray(x, np.float32).astype(BF16)


def f64(x):
    return np.asarray(x).astype(np.float64)


B, V, H, CD = 1024, 2048, 1024, 1


def sigmoid(x):
    return 0.5 * (1.0 + np.tanh(0.5 * x))


def setup_inputs():
    s = mx_kscale(B)
    return {"v": bf(np.random.uniform(size=(B, V))),
            "h_p": bf(sigmoid(np.random.standard_normal((B, H)))),
            "u_h0": bf(np.random.uniform(size=(B, H))),
            "vk": bf((np.random.uniform(size=(B, V)) < 0.5) * s[:, None]),
            "hk": bf((np.random.uniform(size=(B, H)) < 0.5) / s[:, None])}


def reference(v, h_p, u_h0, vk, hk):
    h = (f64(h_p) > f64(u_h0)).astype(np.float64)
    w_data_grad = mxq(f64(v).T, 1, "e4m3") @ mxq(h, 0, "e4m3")
    w_model_grad = mxq(f64(vk).T, 1, "e4m3") @ mxq(f64(hk), 0, "e4m3")
    return w_model_grad - w_data_grad

@@ -1,0 +1,192 @@
+from contextlib import ExitStack
+
+import concourse.mybir as mybir
+
+F32 = mybir.dt.float32
+BF16 = mybir.dt.bfloat16
+U32 = mybir.dt.uint32
+U8 = mybir.dt.uint8
+FP8X4 = mybir.dt.float8_e4m3fn_x4
+ALU = mybir.AluOpType
+ACT = mybir.ActivationFunctionType
+
+P = 128
+PACK = 4
+K_PASS = P * PACK
+BATCH, VIS, HID = 1024, 2048, 1024
+PASSES = BATCH // K_PASS
+UNIT = 512
+N_TILE = 512
+M_TILE = 128
+BLOCK = UNIT // M_TILE
+N_HALVES = HID // N_TILE
+N_BLOCKS = VIS // UNIT
+
+FLOPS = 2 * 2 * BATCH * VIS * HID
+
+PINNED = True
+
+
+def tile_rbm_pb_kernel(tc, v, h_p, u_h0, vk, hk, out):
+    nc = tc.nc
+    with ExitStack() as ctx:
+        raw = ctx.enter_context(tc.tile_pool(name="raw", bufs=1))
+        raw_st = ctx.enter_context(tc.tile_pool(name="raw_st", bufs=8))
+        keep = ctx.enter_context(tc.tile_pool(name="keep", bufs=1))
+        work = ctx.enter_context(tc.tile_pool(name="work", bufs=6))
+        stage = ctx.enter_context(tc.tile_pool(name="stage", bufs=12))
+        psum = ctx.enter_context(tc.psum_pool(name="psum", bufs=8))
+        if PINNED:
+            ctx.enter_context(tc.manual_schedule())
+
+        dram = {"v": v, "vk": vk, "hk": hk, "hp": h_p, "u": u_h0}
+        width = {"v": VIS, "vk": VIS, "hk": HID, "h": HID}
+        codes = {}
+        scales = {}
+        for nm in ("v", "vk", "hk", "h"):
+            codes[nm] = keep.tile([P, PASSES, width[nm]], U32, name="codes_" + nm, align_bytes=64)
+            scales[nm] = keep.tile([P, PASSES, width[nm]], U8, name="scales_" + nm, align_bytes=64)
+
+        raws = {}
+
+        def load(nm, c, col0, cols):
+            if cols == UNIT:
+                t = raw_st.tile([P, PACK, cols], BF16, name="raw_unit", align_bytes=64)
+            else:
+                t = raw.tile([P, PACK, cols], BF16, name="raw_%s_%d" % (nm, c), align_bytes=64)
+            src = dram[nm][c * K_PASS:(c + 1) * K_PASS, col0:col0 + cols]
+            nc.sync.dma_start(out=t[:], in_=src.rearrange("(p j) w -> p j w", j=PACK))
+            raws[(nm, c, col0)] = t
+
+        def load_block(b):
+            for nm in ("vk", "v"):
+                for c in range(PASSES):
+                    load(nm, c, b * UNIT, UNIT)
+
+        def regroup(engine, src, negate=False):
+            grouped = work.tile([P, UNIT, PACK], BF16, name="grouped", align_bytes=64)
+            d = grouped[:].rearrange("p (c i) t -> p c t i", i=4)
+            s = src.rearrange("p t (c i) -> p c t i", i=4)
+            if engine == "v":
+                if negate:
+                    nc.vector.tensor_scalar(out=d, in0=s, scalar1=-1.0, scalar2=None, op0=ALU.mult)
+                else:
+                    nc.vector.tensor_copy(out=d, in_=s)
+            else:
+                if negate:
+                    nc.scalar.activation(out=d, in_=s, func=ACT.Copy, scale=-1.0)
+                else:
+                    nc.scalar.copy(out=d, in_=s)
+            return grouped
+
+        def quantise(nm, c, col0, grouped):
+            nc.vector.quantize_mx(
+                out=codes[nm][:, c, col0:col0 + UNIT].bitcast(FP8X4),
+                scales=scales[nm][:, c, col0:col0 + UNIT],
+                in_=grouped[:].rearrange("p w j -> p (w j)"),
+            )
+
+        def half_of(nm, c, half):
+            return raws[(nm, c, 0)][:, :, half * UNIT:(half + 1) * UNIT]
+
+        def compare(c, half):
+            nc.vector.tensor_tensor(out=half_of("hp", c, half), in0=half_of("hp", c, half),
+                                    in1=half_of("u", c, half), op=ALU.is_gt)
+
+        for c in range(PASSES):
+            load("vk", c, 0, UNIT)
+            load("hk", c, 0, HID)
+            load("hp", c, 0, HID)
+            load("u", c, 0, HID)
+            load("v", c, 0, UNIT)
+        load_block(1)
+
+        g_v = None
+        waiting = None
+        for c in range(PASSES):
+            last = c == PASSES - 1
+            g_vk = regroup("s", raws[("vk", c, 0)][:])
+            g_hk0 = regroup("v", half_of("hk", c, 0))
+            g_hk1 = regroup("s", half_of("hk", c, 1))
+            if c:
+                quantise("v", c - 1, 0, g_v)
+            quantise("hk", c, 0, g_hk0)
+            quantise("hk", c, UNIT, g_hk1)
+            quantise("vk", c, 0, g_vk)
+            compare(c, 0)
+            compare(c, 1)
+            g_h0 = regroup("v", half_of("hp", c, 0), negate=True)
+            g_v = regroup("s", raws[("v", c, 0)][:])
+            g_h1 = regroup("s" if last else "v", half_of("hp", c, 1), negate=True)
+            if last:
+                quantise("v", c, 0, g_v)
+            quantise("h", c, 0, g_h0)
+            if last:
+                waiting = ("h", c, UNIT, g_h1)
+            else:
+                quantise("h", c, UNIT, g_h1)
+
+        for b in range(1, N_BLOCKS):
+            if b + 1 < N_BLOCKS:
+                load_block(b + 1)
+            for nm in ("vk", "v"):
+                for c in range(PASSES):
+                    g = regroup("v", raws[(nm, c, b * UNIT)][:])
+                    quantise(*waiting)
+                    waiting = (nm, c, b * UNIT, g)
+        quantise(*waiting)
+
+        moving_of = {"vk": "hk", "v": "h"}
+
+        def mx_pass(acc, nm, c, m, half, start, stop):
+            mv = moving_of[nm]
+            m_cols = slice(m * M_TILE, (m + 1) * M_TILE)
+            n_cols = slice(half * N_TILE, (half + 1) * N_TILE)
+            nc.tensor.matmul_mx(
+                out=acc[:],
+                lhsT=codes[nm][:, c, m_cols].bitcast(FP8X4),
+                lhsT_scale=scales[nm][:, c, m_cols],
+                rhs=codes[mv][:, c, n_cols].bitcast(FP8X4),
+                rhs_scale=scales[mv][:, c, n_cols],
+                start=start,
+                stop=stop,
+            )
+
+        for b in range(N_BLOCKS):
+            tiles = [b * BLOCK + i for i in range(BLOCK)]
+            if b == 0:
+                groups = [(m, half) for half in range(N_HALVES) for m in tiles]
+            else:
+                groups = [(m, half) for m in tiles for half in range(N_HALVES)]
+            accs = {}
+            results = {}
+            for g in groups:
+                accs[g] = psum.tile([P, N_TILE], F32, name="acc")
+            for m in tiles:
+                results[m] = stage.tile([P, HID], F32, name="result")
+
+            def leave(g):
+                m, half = g
+                n_cols = slice(half * N_TILE, (half + 1) * N_TILE)
+                nc.scalar.copy(out=results[m][:, n_cols], in_=accs[g][:])
+                rows = slice(m * M_TILE, (m + 1) * M_TILE)
+                if m == VIS // M_TILE - 1:
+                    nc.sync.dma_start(out=out[rows, n_cols], in_=results[m][:, n_cols])
+                elif half == N_HALVES - 1:
+                    nc.sync.dma_start(out=out[rows, :], in_=results[m][:])
+
+            if b == 0:
+                order = [("vk", 0), ("v", 0), ("vk", 1), ("v", 1)]
+                for t, (nm, c) in enumerate(order):
+                    for g in groups:
+                        mx_pass(accs[g], nm, c, g[0], g[1], t == 0, t == len(order) - 1)
+                for g in groups:
+                    leave(g)
+            else:
+                for c in range(PASSES):
+                    for g in groups:
+                        mx_pass(accs[g], "vk", c, g[0], g[1], c == 0, False)
+                for g in groups:
+                    for c in range(PASSES):
+                        mx_pass(accs[g], "v", c, g[0], g[1], False, c == PASSES - 1)
+                    leave(g)

@@ -129,19 +129,26 @@ def tile_rbm_pb_kernel(tc, v, h_p, u_h0, vk, hk, out):
         for b in range(1, N_BLOCKS):
             if b + 1 < N_BLOCKS:
                 load_block(b + 1)
-            for nm in ("vk", "v"):
-                for c in range(PASSES):
-                    g = regroup("v", raws[(nm, c, b * UNIT)][:])
+            units = [(nm, c) for nm in ("vk", "v") for c in range(PASSES)]
+            ready = []
+            for i, (nm, c) in enumerate(units):
+                ready.append((nm, c, b * UNIT, regroup("v", raws[(nm, c, b * UNIT)][:])))
+                if waiting is not None:
                     quantise(*waiting)
-                    waiting = (nm, c, b * UNIT, g)
-        quantise(*waiting)
+                    waiting = None
+                if i == 0:
+                    quantise(*ready[0])
+                elif i >= 2:
+                    quantise(*ready[i - 1])
+            quantise(*ready[len(units) - 1])
 
         moving_of = {"vk": "hk", "v": "h"}
 
-        def mx_pass(acc, nm, c, m, half, start, stop):
+        def mx_pass(acc, nm, c, g, start, stop):
+            m, n0, n_len = g
             mv = moving_of[nm]
             m_cols = slice(m * M_TILE, (m + 1) * M_TILE)
-            n_cols = slice(half * N_TILE, (half + 1) * N_TILE)
+            n_cols = slice(n0, n0 + n_len)
             nc.tensor.matmul_mx(
                 out=acc[:],
                 lhsT=codes[nm][:, c, m_cols].bitcast(FP8X4),
@@ -152,41 +159,56 @@ def tile_rbm_pb_kernel(tc, v, h_p, u_h0, vk, hk, out):
                 stop=stop,
             )
 
+        last_m = VIS // M_TILE - 1
         for b in range(N_BLOCKS):
             tiles = [b * BLOCK + i for i in range(BLOCK)]
             if b == 0:
-                groups = [(m, half) for half in range(N_HALVES) for m in tiles]
+                groups = [(m, half * N_TILE, N_TILE) for half in range(N_HALVES) for m in tiles]
             else:
-                groups = [(m, half) for m in tiles for half in range(N_HALVES)]
+                groups = [(m, half * N_TILE, N_TILE) for m in tiles for half in range(N_HALVES)]
+            tail_group = None
+            if b == N_BLOCKS - 1:
+                groups[len(groups) - 1] = (last_m, HID - N_TILE, N_TILE // 2)
+                tail_group = (last_m, HID - N_TILE // 2, N_TILE // 2)
             accs = {}
             results = {}
             for g in groups:
-                accs[g] = psum.tile([P, N_TILE], F32, name="acc")
+                accs[g] = psum.tile([P, g[2]], F32, name="acc")
             for m in tiles:
                 results[m] = stage.tile([P, HID], F32, name="result")
 
-            def leave(g):
-                m, half = g
-                n_cols = slice(half * N_TILE, (half + 1) * N_TILE)
-                nc.scalar.copy(out=results[m][:, n_cols], in_=accs[g][:])
+            def leave(g, engine):
+                m, n0, n_len = g
+                n_cols = slice(n0, n0 + n_len)
+                if engine == "v":
+                    nc.vector.tensor_copy(out=results[m][:, n_cols], in_=accs[g][:])
+                else:
+                    nc.scalar.copy(out=results[m][:, n_cols], in_=accs[g][:])
                 rows = slice(m * M_TILE, (m + 1) * M_TILE)
-                if m == VIS // M_TILE - 1:
+                if m == last_m:
                     nc.sync.dma_start(out=out[rows, n_cols], in_=results[m][:, n_cols])
-                elif half == N_HALVES - 1:
+                elif n0 + n_len == HID:
                     nc.sync.dma_start(out=out[rows, :], in_=results[m][:])
 
             if b == 0:
                 order = [("vk", 0), ("v", 0), ("vk", 1), ("v", 1)]
                 for t, (nm, c) in enumerate(order):
                     for g in groups:
-                        mx_pass(accs[g], nm, c, g[0], g[1], t == 0, t == len(order) - 1)
+                        mx_pass(accs[g], nm, c, g, t == 0, t == len(order) - 1)
                 for g in groups:
-                    leave(g)
+                    leave(g, "s")
             else:
                 for c in range(PASSES):
                     for g in groups:
-                        mx_pass(accs[g], "vk", c, g[0], g[1], c == 0, False)
+                        mx_pass(accs[g], "vk", c, g, c == 0, False)
                 for g in groups:
                     for c in range(PASSES):
-                        mx_pass(accs[g], "v", c, g[0], g[1], False, c == PASSES - 1)
-                    leave(g)
+                        mx_pass(accs[g], "v", c, g, False, c == PASSES - 1)
+                    leave(g, "s")
+            if tail_group is not None:
+                accs[tail_group] = psum.tile([P, tail_group[2]], F32, name="acc")
+                for nm in ("vk", "v"):
+                    for c in range(PASSES):
+                        mx_pass(accs[tail_group], nm, c, tail_group, nm == "vk" and c == 0,
+                                nm == "v" and c == PASSES - 1)
+                leave(tail_group, "v")

@@ -25,12 +25,13 @@ N_BLOCKS = VIS // UNIT
 FLOPS = 2 * 2 * BATCH * VIS * HID
 
 PINNED = True
+WIDE_FROM = 2
 
 
 def tile_rbm_pb_kernel(tc, v, h_p, u_h0, vk, hk, out):
     nc = tc.nc
     with ExitStack() as ctx:
-        raw = ctx.enter_context(tc.tile_pool(name="raw", bufs=1))
+        raw = ctx.enter_context(tc.tile_pool(name="raw", bufs=6))
         raw_st = ctx.enter_context(tc.tile_pool(name="raw_st", bufs=8))
         keep = ctx.enter_context(tc.tile_pool(name="keep", bufs=1))
         work = ctx.enter_context(tc.tile_pool(name="work", bufs=6))
@@ -53,15 +54,20 @@ def tile_rbm_pb_kernel(tc, v, h_p, u_h0, vk, hk, out):
             if cols == UNIT:
                 t = raw_st.tile([P, PACK, cols], BF16, name="raw_unit", align_bytes=64)
             else:
-                t = raw.tile([P, PACK, cols], BF16, name="raw_%s_%d" % (nm, c), align_bytes=64)
+                t = raw.tile([P, PACK, cols], BF16, name="raw_wide", align_bytes=64)
             src = dram[nm][c * K_PASS:(c + 1) * K_PASS, col0:col0 + cols]
             nc.sync.dma_start(out=t[:], in_=src.rearrange("(p j) w -> p j w", j=PACK))
             raws[(nm, c, col0)] = t
 
-        def load_block(b):
+        def load_block(b, cols):
             for nm in ("vk", "v"):
                 for c in range(PASSES):
-                    load(nm, c, b * UNIT, UNIT)
+                    load(nm, c, b * UNIT, cols)
+
+        def unit_of(nm, c, b):
+            if b < WIDE_FROM:
+                return raws[(nm, c, b * UNIT)][:]
+            return raws[(nm, c, WIDE_FROM * UNIT)][:, :, (b - WIDE_FROM) * UNIT:(b - WIDE_FROM + 1) * UNIT]
 
         def regroup(engine, src, negate=False):
             grouped = work.tile([P, UNIT, PACK], BF16, name="grouped", align_bytes=64)
@@ -99,7 +105,7 @@ def tile_rbm_pb_kernel(tc, v, h_p, u_h0, vk, hk, out):
             load("hp", c, 0, HID)
             load("u", c, 0, HID)
             load("v", c, 0, UNIT)
-        load_block(1)
+        load_block(1, UNIT)
 
         g_v = None
         waiting = None
@@ -127,12 +133,12 @@ def tile_rbm_pb_kernel(tc, v, h_p, u_h0, vk, hk, out):
                 quantise("h", c, UNIT, g_h1)
 
         for b in range(1, N_BLOCKS):
-            if b + 1 < N_BLOCKS:
-                load_block(b + 1)
+            if b == 1:
+                load_block(WIDE_FROM, (N_BLOCKS - WIDE_FROM) * UNIT)
             units = [(nm, c) for nm in ("vk", "v") for c in range(PASSES)]
             ready = []
             for i, (nm, c) in enumerate(units):
-                ready.append((nm, c, b * UNIT, regroup("v", raws[(nm, c, b * UNIT)][:])))
+                ready.append((nm, c, b * UNIT, regroup("v", unit_of(nm, c, b))))
                 if waiting is not None:
                     quantise(*waiting)
                     waiting = None

@@ -25,13 +25,13 @@ N_BLOCKS = VIS // UNIT
 FLOPS = 2 * 2 * BATCH * VIS * HID
 
 PINNED = True
-WIDE_FROM = 2
+SHIFT = 48
 
 
 def tile_rbm_pb_kernel(tc, v, h_p, u_h0, vk, hk, out):
     nc = tc.nc
     with ExitStack() as ctx:
-        raw = ctx.enter_context(tc.tile_pool(name="raw", bufs=6))
+        raw = ctx.enter_context(tc.tile_pool(name="raw", bufs=1))
         raw_st = ctx.enter_context(tc.tile_pool(name="raw_st", bufs=8))
         keep = ctx.enter_context(tc.tile_pool(name="keep", bufs=1))
         work = ctx.enter_context(tc.tile_pool(name="work", bufs=6))
@@ -44,9 +44,11 @@ def tile_rbm_pb_kernel(tc, v, h_p, u_h0, vk, hk, out):
         width = {"v": VIS, "vk": VIS, "hk": HID, "h": HID}
         codes = {}
         scales = {}
+        shift = {"v": SHIFT, "vk": SHIFT, "hk": 0, "h": 0}
         for nm in ("v", "vk", "hk", "h"):
-            codes[nm] = keep.tile([P, PASSES, width[nm]], U32, name="codes_" + nm, align_bytes=64)
-            scales[nm] = keep.tile([P, PASSES, width[nm]], U8, name="scales_" + nm, align_bytes=64)
+            pad = 64 if shift[nm] else 0
+            codes[nm] = keep.tile([P, PASSES, width[nm] + pad], U32, name="codes_" + nm, align_bytes=256)
+            scales[nm] = keep.tile([P, PASSES, width[nm]], U8, name="scales_" + nm, align_bytes=256)
 
         raws = {}
 
@@ -54,20 +56,15 @@ def tile_rbm_pb_kernel(tc, v, h_p, u_h0, vk, hk, out):
             if cols == UNIT:
                 t = raw_st.tile([P, PACK, cols], BF16, name="raw_unit", align_bytes=64)
             else:
-                t = raw.tile([P, PACK, cols], BF16, name="raw_wide", align_bytes=64)
+                t = raw.tile([P, PACK, cols], BF16, name="raw_%s_%d" % (nm, c), align_bytes=64)
             src = dram[nm][c * K_PASS:(c + 1) * K_PASS, col0:col0 + cols]
             nc.sync.dma_start(out=t[:], in_=src.rearrange("(p j) w -> p j w", j=PACK))
             raws[(nm, c, col0)] = t
 
-        def load_block(b, cols):
+        def load_block(b):
             for nm in ("vk", "v"):
                 for c in range(PASSES):
-                    load(nm, c, b * UNIT, cols)
-
-        def unit_of(nm, c, b):
-            if b < WIDE_FROM:
-                return raws[(nm, c, b * UNIT)][:]
-            return raws[(nm, c, WIDE_FROM * UNIT)][:, :, (b - WIDE_FROM) * UNIT:(b - WIDE_FROM + 1) * UNIT]
+                    load(nm, c, b * UNIT, UNIT)
 
         def regroup(engine, src, negate=False):
             grouped = work.tile([P, UNIT, PACK], BF16, name="grouped", align_bytes=64)
@@ -87,7 +84,7 @@ def tile_rbm_pb_kernel(tc, v, h_p, u_h0, vk, hk, out):
 
         def quantise(nm, c, col0, grouped):
             nc.vector.quantize_mx(
-                out=codes[nm][:, c, col0:col0 + UNIT].bitcast(FP8X4),
+                out=codes[nm][:, c, shift[nm] + col0:shift[nm] + col0 + UNIT].bitcast(FP8X4),
                 scales=scales[nm][:, c, col0:col0 + UNIT],
                 in_=grouped[:].rearrange("p w j -> p (w j)"),
             )
@@ -105,7 +102,7 @@ def tile_rbm_pb_kernel(tc, v, h_p, u_h0, vk, hk, out):
             load("hp", c, 0, HID)
             load("u", c, 0, HID)
             load("v", c, 0, UNIT)
-        load_block(1, UNIT)
+        load_block(1)
 
         g_v = None
         waiting = None
@@ -133,12 +130,12 @@ def tile_rbm_pb_kernel(tc, v, h_p, u_h0, vk, hk, out):
                 quantise("h", c, UNIT, g_h1)
 
         for b in range(1, N_BLOCKS):
-            if b == 1:
-                load_block(WIDE_FROM, (N_BLOCKS - WIDE_FROM) * UNIT)
+            if b + 1 < N_BLOCKS:
+                load_block(b + 1)
             units = [(nm, c) for nm in ("vk", "v") for c in range(PASSES)]
             ready = []
             for i, (nm, c) in enumerate(units):
-                ready.append((nm, c, b * UNIT, regroup("v", unit_of(nm, c, b))))
+                ready.append((nm, c, b * UNIT, regroup("v", raws[(nm, c, b * UNIT)][:])))
                 if waiting is not None:
                     quantise(*waiting)
                     waiting = None
@@ -157,7 +154,7 @@ def tile_rbm_pb_kernel(tc, v, h_p, u_h0, vk, hk, out):
             n_cols = slice(n0, n0 + n_len)
             nc.tensor.matmul_mx(
                 out=acc[:],
-                lhsT=codes[nm][:, c, m_cols].bitcast(FP8X4),
+                lhsT=codes[nm][:, c, SHIFT + m * M_TILE:SHIFT + (m + 1) * M_TILE].bitcast(FP8X4),
                 lhsT_scale=scales[nm][:, c, m_cols],
                 rhs=codes[mv][:, c, n_cols].bitcast(FP8X4),
                 rhs_scale=scales[mv][:, c, n_cols],

from contextlib import ExitStack

import concourse.mybir as mybir

F32 = mybir.dt.float32
BF16 = mybir.dt.bfloat16
U32 = mybir.dt.uint32
U8 = mybir.dt.uint8
FP8X4 = mybir.dt.float8_e4m3fn_x4
ALU = mybir.AluOpType
ACT = mybir.ActivationFunctionType

P = 128
PACK = 4
K_PASS = P * PACK
BATCH, VIS, HID = 1024, 2048, 1024
PASSES = BATCH // K_PASS
UNIT = 512
N_TILE = 512
M_TILE = 128
BLOCK = UNIT // M_TILE
N_HALVES = HID // N_TILE
N_BLOCKS = VIS // UNIT

FLOPS = 2 * 2 * BATCH * VIS * HID

PINNED = True
SHIFT = 48


def tile_rbm_pb_kernel(tc, v, h_p, u_h0, vk, hk, out):
    nc = tc.nc
    with ExitStack() as ctx:
        raw = ctx.enter_context(tc.tile_pool(name="raw", bufs=1))
        raw_st = ctx.enter_context(tc.tile_pool(name="raw_st", bufs=8))
        keep = ctx.enter_context(tc.tile_pool(name="keep", bufs=1))
        work = ctx.enter_context(tc.tile_pool(name="work", bufs=6))
        stage = ctx.enter_context(tc.tile_pool(name="stage", bufs=12))
        psum = ctx.enter_context(tc.psum_pool(name="psum", bufs=8))
        if PINNED:
            ctx.enter_context(tc.manual_schedule())

        dram = {"v": v, "vk": vk, "hk": hk, "hp": h_p, "u": u_h0}
        width = {"v": VIS, "vk": VIS, "hk": HID, "h": HID}
        codes = {}
        scales = {}
        shift = {"v": SHIFT, "vk": SHIFT, "hk": 0, "h": 0}
        for nm in ("v", "vk", "hk", "h"):
            pad = 64 if shift[nm] else 0
            codes[nm] = keep.tile([P, PASSES, width[nm] + pad], U32, name="codes_" + nm, align_bytes=256)
            scales[nm] = keep.tile([P, PASSES, width[nm]], U8, name="scales_" + nm, align_bytes=256)

        raws = {}

        def load(nm, c, col0, cols):
            if cols == UNIT:
                t = raw_st.tile([P, PACK, cols], BF16, name="raw_unit", align_bytes=64)
            else:
                t = raw.tile([P, PACK, cols], BF16, name="raw_%s_%d" % (nm, c), align_bytes=64)
            src = dram[nm][c * K_PASS:(c + 1) * K_PASS, col0:col0 + cols]
            nc.sync.dma_start(out=t[:], in_=src.rearrange("(p j) w -> p j w", j=PACK))
            raws[(nm, c, col0)] = t

        def load_block(b):
            for nm in ("vk", "v"):
                for c in range(PASSES):
                    load(nm, c, b * UNIT, UNIT)

        def regroup(engine, src, negate=False):
            grouped = work.tile([P, UNIT, PACK], BF16, name="grouped", align_bytes=64)
            d = grouped[:].rearrange("p (c i) t -> p c t i", i=4)
            s = src.rearrange("p t (c i) -> p c t i", i=4)
            if engine == "v":
                if negate:
                    nc.vector.tensor_scalar(out=d, in0=s, scalar1=-1.0, scalar2=None, op0=ALU.mult)
                else:
                    nc.vector.tensor_copy(out=d, in_=s)
            else:
                if negate:
                    nc.scalar.activation(out=d, in_=s, func=ACT.Copy, scale=-1.0)
                else:
                    nc.scalar.copy(out=d, in_=s)
            return grouped

        def quantise(nm, c, col0, grouped):
            nc.vector.quantize_mx(
                out=codes[nm][:, c, shift[nm] + col0:shift[nm] + col0 + UNIT].bitcast(FP8X4),
                scales=scales[nm][:, c, col0:col0 + UNIT],
                in_=grouped[:].rearrange("p w j -> p (w j)"),
            )

        def half_of(nm, c, half):
            return raws[(nm, c, 0)][:, :, half * UNIT:(half + 1) * UNIT]

        def compare(c, half):
            nc.vector.tensor_tensor(out=half_of("hp", c, half), in0=half_of("hp", c, half),
                                    in1=half_of("u", c, half), op=ALU.is_gt)

        for c in range(PASSES):
            load("vk", c, 0, UNIT)
            load("hk", c, 0, HID)
            load("hp", c, 0, HID)
            load("u", c, 0, HID)
            load("v", c, 0, UNIT)
        load_block(1)

        g_v = None
        waiting = None
        for c in range(PASSES):
            last = c == PASSES - 1
            g_vk = regroup("s", raws[("vk", c, 0)][:])
            g_hk0 = regroup("v", half_of("hk", c, 0))
            g_hk1 = regroup("s", half_of("hk", c, 1))
            if c:
                quantise("v", c - 1, 0, g_v)
            quantise("hk", c, 0, g_hk0)
            quantise("hk", c, UNIT, g_hk1)
            quantise("vk", c, 0, g_vk)
            compare(c, 0)
            compare(c, 1)
            g_h0 = regroup("v", half_of("hp", c, 0), negate=True)
            g_v = regroup("s", raws[("v", c, 0)][:])
            g_h1 = regroup("s" if last else "v", half_of("hp", c, 1), negate=True)
            if last:
                quantise("v", c, 0, g_v)
            quantise("h", c, 0, g_h0)
            if last:
                waiting = ("h", c, UNIT, g_h1)
            else:
                quantise("h", c, UNIT, g_h1)

        for b in range(1, N_BLOCKS):
            if b + 1 < N_BLOCKS:
                load_block(b + 1)
            units = [(nm, c) for nm in ("vk", "v") for c in range(PASSES)]
            ready = []
            for i, (nm, c) in enumerate(units):
                ready.append((nm, c, b * UNIT, regroup("v", raws[(nm, c, b * UNIT)][:])))
                if waiting is not None:
                    quantise(*waiting)
                    waiting = None
                if i == 0:
                    quantise(*ready[0])
                elif i >= 2:
                    quantise(*ready[i - 1])
            quantise(*ready[len(units) - 1])

        moving_of = {"vk": "hk", "v": "h"}

        def mx_pass(acc, nm, c, g, start, stop):
            m, n0, n_len = g
            mv = moving_of[nm]
            m_cols = slice(m * M_TILE, (m + 1) * M_TILE)
            n_cols = slice(n0, n0 + n_len)
            nc.tensor.matmul_mx(
                out=acc[:],
                lhsT=codes[nm][:, c, SHIFT + m * M_TILE:SHIFT + (m + 1) * M_TILE].bitcast(FP8X4),
                lhsT_scale=scales[nm][:, c, m_cols],
                rhs=codes[mv][:, c, n_cols].bitcast(FP8X4),
                rhs_scale=scales[mv][:, c, n_cols],
                start=start,
                stop=stop,
            )

        last_m = VIS // M_TILE - 1
        for b in range(N_BLOCKS):
            tiles = [b * BLOCK + i for i in range(BLOCK)]
            if b == 0:
                groups = [(m, half * N_TILE, N_TILE) for half in range(N_HALVES) for m in tiles]
            else:
                groups = [(m, half * N_TILE, N_TILE) for m in tiles for half in range(N_HALVES)]
            tail_group = None
            if b == N_BLOCKS - 1:
                groups[len(groups) - 1] = (last_m, HID - N_TILE, N_TILE // 2)
                tail_group = (last_m, HID - N_TILE // 2, N_TILE // 2)
            accs = {}
            results = {}
            for g in groups:
                accs[g] = psum.tile([P, g[2]], F32, name="acc")
            for m in tiles:
                results[m] = stage.tile([P, HID], F32, name="result")

            def leave(g, engine):
                m, n0, n_len = g
                n_cols = slice(n0, n0 + n_len)
                if engine == "v":
                    nc.vector.tensor_copy(out=results[m][:, n_cols], in_=accs[g][:])
                else:
                    nc.scalar.copy(out=results[m][:, n_cols], in_=accs[g][:])
                rows = slice(m * M_TILE, (m + 1) * M_TILE)
                if m == last_m:
                    nc.sync.dma_start(out=out[rows, n_cols], in_=results[m][:, n_cols])
                elif n0 + n_len == HID:
                    nc.sync.dma_start(out=out[rows, :], in_=results[m][:])

            if b == 0:
                order = [("vk", 0), ("v", 0), ("vk", 1), ("v", 1)]
                for t, (nm, c) in enumerate(order):
                    for g in groups:
                        mx_pass(accs[g], nm, c, g, t == 0, t == len(order) - 1)
                for g in groups:
                    leave(g, "s")
            else:
                for c in range(PASSES):
                    for g in groups:
                        mx_pass(accs[g], "vk", c, g, c == 0, False)
                for g in groups:
                    for c in range(PASSES):
                        mx_pass(accs[g], "v", c, g, False, c == PASSES - 1)
                    leave(g, "s")
            if tail_group is not None:
                accs[tail_group] = psum.tile([P, tail_group[2]], F32, name="acc")
                for nm in ("vk", "v"):
                    for c in range(PASSES):
                        mx_pass(accs[tail_group], nm, c, tail_group, nm == "vk" and c == 0,
                                nm == "v" and c == PASSES - 1)
                leave(tail_group, "v")
